import numpy as np
import ml_dtypes

BF16 = ml_dtypes.bfloat16


def bf(x):
    return np.asarray(x, np.float32).astype(BF16)


def f32(x):
    return np.asarray(x, np.float32)


def f64(x):
    return np.asarray(x).astype(np.float64)


def striped(idx):
    return np.tile(idx.reshape(-1, 16).T, (8, 1))


S, D, F, E, R, KN, H, N = 256, 128, 128, 128, 2, 4, 128, 2048
V = 0.15


def setup_inputs():
    return {"table": bf(np.random.standard_normal((S, D))), "w": bf(np.random.uniform(-V, V, (D, R * F))), "kw": bf(np.random.uniform(-V, V, (F, R * E))), "offs": striped(np.concatenate([np.random.permutation(S)[:H] for _ in range(N // H)]))}


def reference(table, w, kw, offs):
    idx = offs[:16].T.reshape(-1)
    t = f64(table)[idx].T
    P = N // R
    hn = np.concatenate([f64(w)[:, r * F:(r + 1) * F].T @ t[:, r * P:(r + 1) * P] for r in range(R)], axis=1)
    hk = np.concatenate([f64(kw)[:, r * E:(r + 1) * E].T @ hn[:, r * P:(r + 1) * P] for r in range(R)], axis=1)
    return np.concatenate([hn, hk], axis=0)

@@ -1,0 +1,77 @@
+import concourse.mybir as mybir
+from concourse.masks import make_identity
+
+BF16, F32, U16 = mybir.dt.bfloat16, mybir.dt.float32, mybir.dt.uint16
+
+P = 128
+NODES = 256
+ENTRIES = 2048
+PER_RELATION = 1024
+PIECE = 256
+CHUNK = 512
+
+FLOPS = 2 * 2 * P * P * ENTRIES
+
+
+def copy_out_of_psum(nc, c, dst, src):
+    if c % 2 == 0:
+        nc.vector.tensor_copy(dst, src)
+    else:
+        nc.scalar.copy(dst, src)
+
+
+def tile_deepudi_kernel(tc, table, w, kw, offs, out):
+    nc = tc.nc
+    chunks = range(ENTRIES // CHUNK)
+    with (
+        tc.tile_pool(name="held", bufs=1) as held,
+        tc.psum_pool(name="flip", bufs=1) as flip,
+        tc.psum_pool(name="hn_banks", bufs=1) as hn_banks,
+        tc.psum_pool(name="hk_banks", bufs=3) as hk_banks,
+    ):
+        offsets = held.tile([P, ENTRIES // 16], U16, name="offsets")
+        nc.sync.dma_start(offsets[:], offs)
+        node_rows = held.tile([P, NODES // P, P], BF16, name="node_rows")
+        nc.scalar.dma_start(node_rows[:], table.rearrange("(b p) d -> p b d", p=P))
+        w_sb = held.tile([P, 2 * P], BF16, name="w_sb")
+        nc.sync.dma_start(w_sb[:], w)
+        kw_sb = held.tile([P, 2 * P], BF16, name="kw_sb")
+        nc.scalar.dma_start(kw_sb[:], kw)
+
+        identity = held.tile([P, P], BF16, name="identity")
+        make_identity(nc, identity[:])
+        flipped = flip.tile([P, NODES], BF16, name="flipped")
+        for b in range(NODES // P):
+            nc.tensor.transpose(flipped[:, b * P : (b + 1) * P], node_rows[:, b, :], identity[:])
+        window = held.tile([P, NODES], BF16, name="window")
+        nc.vector.tensor_copy(window[:], flipped[:])
+
+        hn_psum = [hn_banks.tile([P, CHUNK], F32, name=f"hn_psum{c}") for c in chunks]
+        for c in chunks:
+            r = c * CHUNK // PER_RELATION
+            for h in range(CHUNK // PIECE):
+                first = (c * CHUNK + h * PIECE) // 16
+                nc.tensor.matmul(
+                    hn_psum[c][:, h * PIECE : (h + 1) * PIECE],
+                    w_sb[:, r * P : (r + 1) * P],
+                    window[:].indirect(offsets[:, first : first + PIECE // 16]),
+                    start=True,
+                    stop=True,
+                )
+
+        hn_f32 = held.tile([P, ENTRIES], F32, name="hn_f32")
+        hn_bf16 = held.tile([P, ENTRIES], BF16, name="hn_bf16")
+        for c in chunks:
+            cols = slice(c * CHUNK, (c + 1) * CHUNK)
+            copy_out_of_psum(nc, c, hn_f32[:, cols], hn_psum[c][:])
+            nc.sync.dma_start(out[0:P, cols], hn_f32[:, cols])
+            copy_out_of_psum(nc, c, hn_bf16[:, cols], hn_psum[c][:])
+
+        hk_f32 = held.tile([P, ENTRIES], F32, name="hk_f32")
+        for c in chunks:
+            r = c * CHUNK // PER_RELATION
+            cols = slice(c * CHUNK, (c + 1) * CHUNK)
+            hk_psum = hk_banks.tile([P, CHUNK], F32, name="hk_psum")
+            nc.tensor.matmul(hk_psum[:], kw_sb[:, r * P : (r + 1) * P], hn_bf16[:, cols], start=True, stop=True)
+            copy_out_of_psum(nc, c, hk_f32[:, cols], hk_psum[:])
+            nc.sync.dma_start(out[P : 2 * P, cols], hk_f32[:, cols])

@@ -9,6 +9,7 @@ ENTRIES = 2048
 PER_RELATION = 1024
 PIECE = 256
 CHUNK = 512
+WARM_UPS = 6
 
 FLOPS = 2 * 2 * P * P * ENTRIES
 
@@ -38,6 +39,12 @@ def tile_deepudi_kernel(tc, table, w, kw, offs, out):
         kw_sb = held.tile([P, 2 * P], BF16, name="kw_sb")
         nc.scalar.dma_start(kw_sb[:], kw)
 
+        hn_psum = [hn_banks.tile([P, CHUNK], F32, name=f"hn_psum{c}") for c in chunks]
+        zeros = held.tile([P, CHUNK], BF16, name="zeros")
+        nc.vector.memset(zeros[:], 0.0)
+        for i in range(WARM_UPS):
+            nc.tensor.matmul(hn_psum[-1][:], zeros[:, 0:P], zeros[:], start=True, stop=True)
+
         identity = held.tile([P, P], BF16, name="identity")
         make_identity(nc, identity[:])
         flipped = flip.tile([P, NODES], BF16, name="flipped")
@@ -46,7 +53,6 @@ def tile_deepudi_kernel(tc, table, w, kw, offs, out):
         window = held.tile([P, NODES], BF16, name="window")
         nc.vector.tensor_copy(window[:], flipped[:])
 
-        hn_psum = [hn_banks.tile([P, CHUNK], F32, name=f"hn_psum{c}") for c in chunks]
         for c in chunks:
             r = c * CHUNK // PER_RELATION
             for h in range(CHUNK // PIECE):

@@ -9,7 +9,6 @@ ENTRIES = 2048
 PER_RELATION = 1024
 PIECE = 256
 CHUNK = 512
-WARM_UPS = 6
 
 FLOPS = 2 * 2 * P * P * ENTRIES
 
@@ -24,60 +23,56 @@ def copy_out_of_psum(nc, c, dst, src):
 def tile_deepudi_kernel(tc, table, w, kw, offs, out):
     nc = tc.nc
     chunks = range(ENTRIES // CHUNK)
-    with (
-        tc.tile_pool(name="held", bufs=1) as held,
-        tc.psum_pool(name="flip", bufs=1) as flip,
-        tc.psum_pool(name="hn_banks", bufs=1) as hn_banks,
-        tc.psum_pool(name="hk_banks", bufs=3) as hk_banks,
-    ):
+    with tc.tile_pool(name="held", bufs=1) as held:
+        node_rows = [held.tile([P, P], BF16, name=f"node_rows{b}") for b in range(NODES // P)]
+        nc.sync.dma_start(node_rows[0][:], table[0:P, :])
+        nc.scalar.dma_start(node_rows[1][:], table[P : 2 * P, :])
         offsets = held.tile([P, ENTRIES // 16], U16, name="offsets")
         nc.sync.dma_start(offsets[:], offs)
-        node_rows = held.tile([P, NODES // P, P], BF16, name="node_rows")
-        nc.scalar.dma_start(node_rows[:], table.rearrange("(b p) d -> p b d", p=P))
         w_sb = held.tile([P, 2 * P], BF16, name="w_sb")
-        nc.sync.dma_start(w_sb[:], w)
+        nc.scalar.dma_start(w_sb[:], w)
         kw_sb = held.tile([P, 2 * P], BF16, name="kw_sb")
-        nc.scalar.dma_start(kw_sb[:], kw)
-
-        hn_psum = [hn_banks.tile([P, CHUNK], F32, name=f"hn_psum{c}") for c in chunks]
-        zeros = held.tile([P, CHUNK], BF16, name="zeros")
-        nc.vector.memset(zeros[:], 0.0)
-        for i in range(WARM_UPS):
-            nc.tensor.matmul(hn_psum[-1][:], zeros[:, 0:P], zeros[:], start=True, stop=True)
+        nc.sync.dma_start(kw_sb[:], kw)
 
         identity = held.tile([P, P], BF16, name="identity")
         make_identity(nc, identity[:])
-        flipped = flip.tile([P, NODES], BF16, name="flipped")
-        for b in range(NODES // P):
-            nc.tensor.transpose(flipped[:, b * P : (b + 1) * P], node_rows[:, b, :], identity[:])
         window = held.tile([P, NODES], BF16, name="window")
-        nc.vector.tensor_copy(window[:], flipped[:])
+        with tc.psum_pool(name="flip", bufs=1) as flip:
+            for b in range(NODES // P):
+                flipped = flip.tile([P, P], BF16, name=f"flipped{b}")
+                nc.tensor.transpose(flipped[:], node_rows[b][:], identity[:])
+                copy_out_of_psum(nc, b, window[:, b * P : (b + 1) * P], flipped[:])
 
-        for c in chunks:
-            r = c * CHUNK // PER_RELATION
-            for h in range(CHUNK // PIECE):
-                first = (c * CHUNK + h * PIECE) // 16
-                nc.tensor.matmul(
-                    hn_psum[c][:, h * PIECE : (h + 1) * PIECE],
-                    w_sb[:, r * P : (r + 1) * P],
-                    window[:].indirect(offsets[:, first : first + PIECE // 16]),
-                    start=True,
-                    stop=True,
-                )
+        with (
+            tc.psum_pool(name="hn_banks", bufs=1) as hn_banks,
+            tc.psum_pool(name="hk_banks", bufs=3) as hk_banks,
+        ):
+            hn_psum = [hn_banks.tile([P, CHUNK], F32, name=f"hn_psum{c}") for c in chunks]
+            for c in chunks:
+                r = c * CHUNK // PER_RELATION
+                for h in range(CHUNK // PIECE):
+                    first = (c * CHUNK + h * PIECE) // 16
+                    nc.tensor.matmul(
+                        hn_psum[c][:, h * PIECE : (h + 1) * PIECE],
+                        w_sb[:, r * P : (r + 1) * P],
+                        window[:].indirect(offsets[:, first : first + PIECE // 16]),
+                        start=True,
+                        stop=True,
+                    )
 
-        hn_f32 = held.tile([P, ENTRIES], F32, name="hn_f32")
-        hn_bf16 = held.tile([P, ENTRIES], BF16, name="hn_bf16")
-        for c in chunks:
-            cols = slice(c * CHUNK, (c + 1) * CHUNK)
-            copy_out_of_psum(nc, c, hn_f32[:, cols], hn_psum[c][:])
-            nc.sync.dma_start(out[0:P, cols], hn_f32[:, cols])
-            copy_out_of_psum(nc, c, hn_bf16[:, cols], hn_psum[c][:])
+            hn_f32 = held.tile([P, ENTRIES], F32, name="hn_f32")
+            hn_bf16 = held.tile([P, ENTRIES], BF16, name="hn_bf16")
+            for c in chunks:
+                cols = slice(c * CHUNK, (c + 1) * CHUNK)
+                copy_out_of_psum(nc, c, hn_f32[:, cols], hn_psum[c][:])
+                nc.sync.dma_start(out[0:P, cols], hn_f32[:, cols])
+                copy_out_of_psum(nc, c, hn_bf16[:, cols], hn_psum[c][:])
 
-        hk_f32 = held.tile([P, ENTRIES], F32, name="hk_f32")
-        for c in chunks:
-            r = c * CHUNK // PER_RELATION
-            cols = slice(c * CHUNK, (c + 1) * CHUNK)
-            hk_psum = hk_banks.tile([P, CHUNK], F32, name="hk_psum")
-            nc.tensor.matmul(hk_psum[:], kw_sb[:, r * P : (r + 1) * P], hn_bf16[:, cols], start=True, stop=True)
-            copy_out_of_psum(nc, c, hk_f32[:, cols], hk_psum[:])
-            nc.sync.dma_start(out[P : 2 * P, cols], hk_f32[:, cols])
+            hk_f32 = held.tile([P, ENTRIES], F32, name="hk_f32")
+            for c in chunks:
+                r = c * CHUNK // PER_RELATION
+                cols = slice(c * CHUNK, (c + 1) * CHUNK)
+                hk_psum = hk_banks.tile([P, CHUNK], F32, name="hk_psum")
+                nc.tensor.matmul(hk_psum[:], kw_sb[:, r * P : (r + 1) * P], hn_bf16[:, cols], start=True, stop=True)
+                copy_out_of_psum(nc, c, hk_f32[:, cols], hk_psum[:])
+                nc.sync.dma_start(out[P : 2 * P, cols], hk_f32[:, cols])

@@ -9,6 +9,7 @@ ENTRIES = 2048
 PER_RELATION = 1024
 PIECE = 256
 CHUNK = 512
+WARM_UPS = 4
 
 FLOPS = 2 * 2 * P * P * ENTRIES
 
@@ -33,6 +34,13 @@ def tile_deepudi_kernel(tc, table, w, kw, offs, out):
         nc.scalar.dma_start(w_sb[:], w)
         kw_sb = held.tile([P, 2 * P], BF16, name="kw_sb")
         nc.sync.dma_start(kw_sb[:], kw)
+
+        zeros = held.tile([P, PIECE], BF16, name="zeros")
+        nc.vector.memset(zeros[:], 0.0)
+        with tc.psum_pool(name="idle", bufs=1) as idle:
+            unused = idle.tile([P, PIECE], F32, name="unused")
+            for i in range(WARM_UPS):
+                nc.tensor.matmul(unused[:], zeros[:, 0:P], zeros[:], start=True, stop=True)
 
         identity = held.tile([P, P], BF16, name="identity")
         make_identity(nc, identity[:])

@@ -9,7 +9,6 @@ ENTRIES = 2048
 PER_RELATION = 1024
 PIECE = 256
 CHUNK = 512
-WARM_UPS = 4
 
 FLOPS = 2 * 2 * P * P * ENTRIES
 
@@ -19,6 +18,13 @@ def copy_out_of_psum(nc, c, dst, src):
         nc.vector.tensor_copy(dst, src)
     else:
         nc.scalar.copy(dst, src)
+
+
+def store(nc, c, dst, src):
+    if c % 2 == 0:
+        nc.sync.dma_start(dst, src)
+    else:
+        nc.scalar.dma_start(dst, src)
 
 
 def tile_deepudi_kernel(tc, table, w, kw, offs, out):
@@ -34,13 +40,6 @@ def tile_deepudi_kernel(tc, table, w, kw, offs, out):
         nc.scalar.dma_start(w_sb[:], w)
         kw_sb = held.tile([P, 2 * P], BF16, name="kw_sb")
         nc.sync.dma_start(kw_sb[:], kw)
-
-        zeros = held.tile([P, PIECE], BF16, name="zeros")
-        nc.vector.memset(zeros[:], 0.0)
-        with tc.psum_pool(name="idle", bufs=1) as idle:
-            unused = idle.tile([P, PIECE], F32, name="unused")
-            for i in range(WARM_UPS):
-                nc.tensor.matmul(unused[:], zeros[:, 0:P], zeros[:], start=True, stop=True)
 
         identity = held.tile([P, P], BF16, name="identity")
         make_identity(nc, identity[:])
@@ -73,7 +72,7 @@ def tile_deepudi_kernel(tc, table, w, kw, offs, out):
             for c in chunks:
                 cols = slice(c * CHUNK, (c + 1) * CHUNK)
                 copy_out_of_psum(nc, c, hn_f32[:, cols], hn_psum[c][:])
-                nc.sync.dma_start(out[0:P, cols], hn_f32[:, cols])
+                store(nc, c, out[0:P, cols], hn_f32[:, cols])
                 copy_out_of_psum(nc, c, hn_bf16[:, cols], hn_psum[c][:])
 
             hk_f32 = held.tile([P, ENTRIES], F32, name="hk_f32")
@@ -83,4 +82,4 @@ def tile_deepudi_kernel(tc, table, w, kw, offs, out):
                 hk_psum = hk_banks.tile([P, CHUNK], F32, name="hk_psum")
                 nc.tensor.matmul(hk_psum[:], kw_sb[:, r * P : (r + 1) * P], hn_bf16[:, cols], start=True, stop=True)
                 copy_out_of_psum(nc, c, hk_f32[:, cols], hk_psum[:])
-                nc.sync.dma_start(out[P : 2 * P, cols], hk_f32[:, cols])
+                store(nc, c, out[P : 2 * P, cols], hk_f32[:, cols])

@@ -8,20 +8,21 @@ NODES = 256
 ENTRIES = 2048
 PER_RELATION = 1024
 PIECE = 256
-CHUNK = 512
+STORE = 512
+BANKS = 8
 
 FLOPS = 2 * 2 * P * P * ENTRIES
 
 
-def copy_out_of_psum(nc, c, dst, src):
-    if c % 2 == 0:
+def copy_out_of_psum(nc, k, dst, src):
+    if k % 2 == 0:
         nc.vector.tensor_copy(dst, src)
     else:
         nc.scalar.copy(dst, src)
 
 
-def store(nc, c, dst, src):
-    if c % 2 == 0:
+def store(nc, s, dst, src):
+    if s % 2 == 0:
         nc.sync.dma_start(dst, src)
     else:
         nc.scalar.dma_start(dst, src)
@@ -29,7 +30,7 @@ def store(nc, c, dst, src):
 
 def tile_deepudi_kernel(tc, table, w, kw, offs, out):
     nc = tc.nc
-    chunks = range(ENTRIES // CHUNK)
+    pieces = range(ENTRIES // PIECE)
     with tc.tile_pool(name="held", bufs=1) as held:
         node_rows = [held.tile([P, P], BF16, name=f"node_rows{b}") for b in range(NODES // P)]
         nc.sync.dma_start(node_rows[0][:], table[0:P, :])
@@ -50,36 +51,37 @@ def tile_deepudi_kernel(tc, table, w, kw, offs, out):
                 nc.tensor.transpose(flipped[:], node_rows[b][:], identity[:])
                 copy_out_of_psum(nc, b, window[:, b * P : (b + 1) * P], flipped[:])
 
-        with (
-            tc.psum_pool(name="hn_banks", bufs=1) as hn_banks,
-            tc.psum_pool(name="hk_banks", bufs=3) as hk_banks,
-        ):
-            hn_psum = [hn_banks.tile([P, CHUNK], F32, name=f"hn_psum{c}") for c in chunks]
-            for c in chunks:
-                r = c * CHUNK // PER_RELATION
-                for h in range(CHUNK // PIECE):
-                    first = (c * CHUNK + h * PIECE) // 16
-                    nc.tensor.matmul(
-                        hn_psum[c][:, h * PIECE : (h + 1) * PIECE],
-                        w_sb[:, r * P : (r + 1) * P],
-                        window[:].indirect(offsets[:, first : first + PIECE // 16]),
-                        start=True,
-                        stop=True,
-                    )
+        with tc.psum_pool(name="banks", bufs=BANKS) as banks:
+            hn_psum = []
+            for k in pieces:
+                r = k * PIECE // PER_RELATION
+                bank = banks.tile([P, PIECE], F32, name="bank")
+                nc.tensor.matmul(
+                    bank[:],
+                    w_sb[:, r * P : (r + 1) * P],
+                    window[:].indirect(offsets[:, k * PIECE // 16 : (k + 1) * PIECE // 16]),
+                    start=True,
+                    stop=True,
+                )
+                hn_psum.append(bank)
 
             hn_f32 = held.tile([P, ENTRIES], F32, name="hn_f32")
             hn_bf16 = held.tile([P, ENTRIES], BF16, name="hn_bf16")
-            for c in chunks:
-                cols = slice(c * CHUNK, (c + 1) * CHUNK)
-                copy_out_of_psum(nc, c, hn_f32[:, cols], hn_psum[c][:])
-                store(nc, c, out[0:P, cols], hn_f32[:, cols])
-                copy_out_of_psum(nc, c, hn_bf16[:, cols], hn_psum[c][:])
+            for k in pieces:
+                cols = slice(k * PIECE, (k + 1) * PIECE)
+                copy_out_of_psum(nc, k, hn_f32[:, cols], hn_psum[k][:])
+                if (k + 1) * PIECE % STORE == 0:
+                    both = slice((k + 1) * PIECE - STORE, (k + 1) * PIECE)
+                    store(nc, k * PIECE // STORE, out[0:P, both], hn_f32[:, both])
+                copy_out_of_psum(nc, k, hn_bf16[:, cols], hn_psum[k][:])
 
             hk_f32 = held.tile([P, ENTRIES], F32, name="hk_f32")
-            for c in chunks:
-                r = c * CHUNK // PER_RELATION
-                cols = slice(c * CHUNK, (c + 1) * CHUNK)
-                hk_psum = hk_banks.tile([P, CHUNK], F32, name="hk_psum")
-                nc.tensor.matmul(hk_psum[:], kw_sb[:, r * P : (r + 1) * P], hn_bf16[:, cols], start=True, stop=True)
-                copy_out_of_psum(nc, c, hk_f32[:, cols], hk_psum[:])
-                store(nc, c, out[P : 2 * P, cols], hk_f32[:, cols])
+            for k in pieces:
+                r = k * PIECE // PER_RELATION
+                cols = slice(k * PIECE, (k + 1) * PIECE)
+                bank = banks.tile([P, PIECE], F32, name="bank")
+                nc.tensor.matmul(bank[:], kw_sb[:, r * P : (r + 1) * P], hn_bf16[:, cols], start=True, stop=True)
+                copy_out_of_psum(nc, k, hk_f32[:, cols], bank[:])
+                if (k + 1) * PIECE % STORE == 0:
+                    both = slice((k + 1) * PIECE - STORE, (k + 1) * PIECE)
+                    store(nc, k * PIECE // STORE, out[P : 2 * P, both], hk_f32[:, both])

@@ -76,12 +76,15 @@ def tile_deepudi_kernel(tc, table, w, kw, offs, out):
                 copy_out_of_psum(nc, k, hn_bf16[:, cols], hn_psum[k][:])
 
             hk_f32 = held.tile([P, ENTRIES], F32, name="hk_f32")
-            for k in pieces:
-                r = k * PIECE // PER_RELATION
-                cols = slice(k * PIECE, (k + 1) * PIECE)
-                bank = banks.tile([P, PIECE], F32, name="bank")
+            widths = [STORE] * (ENTRIES // STORE - 1) + [STORE // 2] * 2
+            first = 0
+            for k, width in enumerate(widths):
+                r = first // PER_RELATION
+                cols = slice(first, first + width)
+                bank = banks.tile([P, width], F32, name="bank")
                 nc.tensor.matmul(bank[:], kw_sb[:, r * P : (r + 1) * P], hn_bf16[:, cols], start=True, stop=True)
                 copy_out_of_psum(nc, k, hk_f32[:, cols], bank[:])
-                if (k + 1) * PIECE % STORE == 0:
-                    both = slice((k + 1) * PIECE - STORE, (k + 1) * PIECE)
-                    store(nc, k * PIECE // STORE, out[P : 2 * P, both], hk_f32[:, both])
+                first += width
+                if first % STORE == 0:
+                    ready = slice(first - STORE, first)
+                    store(nc, first // STORE - 1, out[P : 2 * P, ready], hk_f32[:, ready])

@@ -21,13 +21,6 @@ def copy_out_of_psum(nc, k, dst, src):
         nc.scalar.copy(dst, src)
 
 
-def store(nc, s, dst, src):
-    if s % 2 == 0:
-        nc.sync.dma_start(dst, src)
-    else:
-        nc.scalar.dma_start(dst, src)
-
-
 def tile_deepudi_kernel(tc, table, w, kw, offs, out):
     nc = tc.nc
     pieces = range(ENTRIES // PIECE)
@@ -72,7 +65,7 @@ def tile_deepudi_kernel(tc, table, w, kw, offs, out):
                 copy_out_of_psum(nc, k, hn_f32[:, cols], hn_psum[k][:])
                 if (k + 1) * PIECE % STORE == 0:
                     both = slice((k + 1) * PIECE - STORE, (k + 1) * PIECE)
-                    store(nc, k * PIECE // STORE, out[0:P, both], hn_f32[:, both])
+                    nc.sync.dma_start(out[0:P, both], hn_f32[:, both])
                 copy_out_of_psum(nc, k, hn_bf16[:, cols], hn_psum[k][:])
 
             hk_f32 = held.tile([P, ENTRIES], F32, name="hk_f32")
@@ -87,4 +80,4 @@ def tile_deepudi_kernel(tc, table, w, kw, offs, out):
                 first += width
                 if first % STORE == 0:
                     ready = slice(first - STORE, first)
-                    store(nc, first // STORE - 1, out[P : 2 * P, ready], hk_f32[:, ready])
+                    nc.sync.dma_start(out[P : 2 * P, ready], hk_f32[:, ready])

@@ -66,7 +66,10 @@ def tile_deepudi_kernel(tc, table, w, kw, offs, out):
                 if (k + 1) * PIECE % STORE == 0:
                     both = slice((k + 1) * PIECE - STORE, (k + 1) * PIECE)
                     nc.sync.dma_start(out[0:P, both], hn_f32[:, both])
-                copy_out_of_psum(nc, k, hn_bf16[:, cols], hn_psum[k][:])
+                if k % 2 == 0:
+                    nc.vector.tensor_copy(hn_bf16[:, cols], hn_psum[k][:])
+                else:
+                    nc.gpsimd.tensor_copy(hn_bf16[:, cols], hn_f32[:, cols])
 
             hk_f32 = held.tile([P, ENTRIES], F32, name="hk_f32")
             widths = [STORE] * (ENTRIES // STORE - 1) + [STORE // 2] * 2
@@ -76,7 +79,7 @@ def tile_deepudi_kernel(tc, table, w, kw, offs, out):
                 cols = slice(first, first + width)
                 bank = banks.tile([P, width], F32, name="bank")
                 nc.tensor.matmul(bank[:], kw_sb[:, r * P : (r + 1) * P], hn_bf16[:, cols], start=True, stop=True)
-                copy_out_of_psum(nc, k, hk_f32[:, cols], bank[:])
+                copy_out_of_psum(nc, k + 1, hk_f32[:, cols], bank[:])
                 first += width
                 if first % STORE == 0:
                     ready = slice(first - STORE, first)

@@ -63,7 +63,9 @@ def tile_deepudi_kernel(tc, table, w, kw, offs, out):
             for k in pieces:
                 cols = slice(k * PIECE, (k + 1) * PIECE)
                 copy_out_of_psum(nc, k, hn_f32[:, cols], hn_psum[k][:])
-                if (k + 1) * PIECE % STORE == 0:
+                if k < 2:
+                    nc.sync.dma_start(out[0:P, cols], hn_f32[:, cols])
+                elif (k + 1) * PIECE % STORE == 0:
                     both = slice((k + 1) * PIECE - STORE, (k + 1) * PIECE)
                     nc.sync.dma_start(out[0:P, both], hn_f32[:, both])
                 if k % 2 == 0:

@@ -75,7 +75,9 @@ def tile_deepudi_kernel(tc, table, w, kw, offs, out):
 
             hk_f32 = held.tile([P, ENTRIES], F32, name="hk_f32")
             widths = [STORE] * (ENTRIES // STORE - 1) + [STORE // 2] * 2
+            store_ends = [STORE, 2 * STORE, ENTRIES]
             first = 0
+            stored = 0
             for k, width in enumerate(widths):
                 r = first // PER_RELATION
                 cols = slice(first, first + width)
@@ -83,6 +85,7 @@ def tile_deepudi_kernel(tc, table, w, kw, offs, out):
                 nc.tensor.matmul(bank[:], kw_sb[:, r * P : (r + 1) * P], hn_bf16[:, cols], start=True, stop=True)
                 copy_out_of_psum(nc, k + 1, hk_f32[:, cols], bank[:])
                 first += width
-                if first % STORE == 0:
-                    ready = slice(first - STORE, first)
+                if first in store_ends:
+                    ready = slice(stored, first)
                     nc.sync.dma_start(out[P : 2 * P, ready], hk_f32[:, ready])
+                    stored = first

@@ -42,7 +42,7 @@ def tile_deepudi_kernel(tc, table, w, kw, offs, out):
             for b in range(NODES // P):
                 flipped = flip.tile([P, P], BF16, name=f"flipped{b}")
                 nc.tensor.transpose(flipped[:], node_rows[b][:], identity[:])
-                copy_out_of_psum(nc, b, window[:, b * P : (b + 1) * P], flipped[:])
+                nc.scalar.copy(window[:, b * P : (b + 1) * P], flipped[:])
 
         with tc.psum_pool(name="banks", bufs=BANKS) as banks:
             hn_psum = []

import concourse.mybir as mybir
from concourse.masks import make_identity

BF16, F32, U16 = mybir.dt.bfloat16, mybir.dt.float32, mybir.dt.uint16

P = 128
NODES = 256
ENTRIES = 2048
PER_RELATION = 1024
PIECE = 256
STORE = 512
BANKS = 8

FLOPS = 2 * 2 * P * P * ENTRIES


def copy_out_of_psum(nc, k, dst, src):
    if k % 2 == 0:
        nc.vector.tensor_copy(dst, src)
    else:
        nc.scalar.copy(dst, src)


def tile_deepudi_kernel(tc, table, w, kw, offs, out):
    nc = tc.nc
    pieces = range(ENTRIES // PIECE)
    with tc.tile_pool(name="held", bufs=1) as held:
        node_rows = [held.tile([P, P], BF16, name=f"node_rows{b}") for b in range(NODES // P)]
        nc.sync.dma_start(node_rows[0][:], table[0:P, :])
        nc.scalar.dma_start(node_rows[1][:], table[P : 2 * P, :])
        offsets = held.tile([P, ENTRIES // 16], U16, name="offsets")
        nc.sync.dma_start(offsets[:], offs)
        w_sb = held.tile([P, 2 * P], BF16, name="w_sb")
        nc.scalar.dma_start(w_sb[:], w)
        kw_sb = held.tile([P, 2 * P], BF16, name="kw_sb")
        nc.sync.dma_start(kw_sb[:], kw)

        identity = held.tile([P, P], BF16, name="identity")
        make_identity(nc, identity[:])
        window = held.tile([P, NODES], BF16, name="window")
        with tc.psum_pool(name="flip", bufs=1) as flip:
            for b in range(NODES // P):
                flipped = flip.tile([P, P], BF16, name=f"flipped{b}")
                nc.tensor.transpose(flipped[:], node_rows[b][:], identity[:])
                nc.scalar.copy(window[:, b * P : (b + 1) * P], flipped[:])

        with tc.psum_pool(name="banks", bufs=BANKS) as banks:
            hn_psum = []
            for k in pieces:
                r = k * PIECE // PER_RELATION
                bank = banks.tile([P, PIECE], F32, name="bank")
                nc.tensor.matmul(
                    bank[:],
                    w_sb[:, r * P : (r + 1) * P],
                    window[:].indirect(offsets[:, k * PIECE // 16 : (k + 1) * PIECE // 16]),
                    start=True,
                    stop=True,
                )
                hn_psum.append(bank)

            hn_f32 = held.tile([P, ENTRIES], F32, name="hn_f32")
            hn_bf16 = held.tile([P, ENTRIES], BF16, name="hn_bf16")
            for k in pieces:
                cols = slice(k * PIECE, (k + 1) * PIECE)
                copy_out_of_psum(nc, k, hn_f32[:, cols], hn_psum[k][:])
                if k < 2:
                    nc.sync.dma_start(out[0:P, cols], hn_f32[:, cols])
                elif (k + 1) * PIECE % STORE == 0:
                    both = slice((k + 1) * PIECE - STORE, (k + 1) * PIECE)
                    nc.sync.dma_start(out[0:P, both], hn_f32[:, both])
                if k % 2 == 0:
                    nc.vector.tensor_copy(hn_bf16[:, cols], hn_psum[k][:])
                else:
                    nc.gpsimd.tensor_copy(hn_bf16[:, cols], hn_f32[:, cols])

            hk_f32 = held.tile([P, ENTRIES], F32, name="hk_f32")
            widths = [STORE] * (ENTRIES // STORE - 1) + [STORE // 2] * 2
            store_ends = [STORE, 2 * STORE, ENTRIES]
            first = 0
            stored = 0
            for k, width in enumerate(widths):
                r = first // PER_RELATION
                cols = slice(first, first + width)
                bank = banks.tile([P, width], F32, name="bank")
                nc.tensor.matmul(bank[:], kw_sb[:, r * P : (r + 1) * P], hn_bf16[:, cols], start=True, stop=True)
                copy_out_of_psum(nc, k + 1, hk_f32[:, cols], bank[:])
                first += width
                if first in store_ends:
                    ready = slice(stored, first)
                    nc.sync.dma_start(out[P : 2 * P, ready], hk_f32[:, ready])
                    stored = first
